import numpy as np
import ml_dtypes

BF16 = ml_dtypes.bfloat16


def bf(x):
    return np.asarray(x, np.float32).astype(BF16)


def f32(x):
    return np.asarray(x, np.float32)


def f64(x):
    return np.asarray(x).astype(np.float64)


def striped(idx):
    return np.tile(idx.reshape(-1, 16).T, (8, 1))


C, C3, S, N, HD, HDL, LD = 512, 1536, 4096, 2048, 32, 8, 128
SCALE = HD ** -0.5
SCALE_L = HDL ** -0.5


def setup_inputs():
    return {
        "x": f32(np.random.standard_normal((C, S))),
        "qkv_w": bf(np.random.standard_normal((C, C3)) / np.sqrt(C)),
        "qkv_b": f32(0.1 * np.random.standard_normal((C3, 1))),
        "ql_w": bf(np.random.standard_normal((C, LD)) / np.sqrt(C)),
        "kl_w": bf(np.random.standard_normal((C, LD)) / np.sqrt(C)),
        "vl_w": bf(np.random.standard_normal((C, LD)) / np.sqrt(C)),
        "offs": striped(np.random.permutation(S)[:N]),
    }


def reference(x, qkv_w, qkv_b, ql_w, kl_w, vl_w, offs):
    idx = offs[:16].T.reshape(-1)
    xp = f64(x)[:, idx]
    qkv = f64(qkv_w).T @ xp + f64(qkv_b)
    qkv[:C] = qkv[:C] * SCALE
    q_l = SCALE_L * (f64(ql_w).T @ xp)
    k_l = f64(kl_w).T @ xp
    v_l = f64(vl_w).T @ xp
    return np.concatenate([qkv, q_l, k_l, v_l], axis=0)

@@ -1,0 +1,112 @@
+import concourse.mybir as mybir
+
+F32 = mybir.dt.float32
+BF16 = mybir.dt.bfloat16
+U16 = mybir.dt.uint16
+COPY = mybir.ActivationFunctionType.Copy
+IDENTITY = mybir.ActivationFunctionType.Identity
+MULT = mybir.AluOpType.mult
+ADD = mybir.AluOpType.add
+
+P = 128
+C = 512
+S = 4096
+N = 2048
+QKV = 1536
+LD = 128
+ROWS = QKV + 3 * LD
+KB = C // P
+MB = ROWS // P
+CHUNK = 512
+NCH = N // CHUNK
+BANKS = 8
+SCALE = 32 ** -0.5
+SCALE_L = 8 ** -0.5
+
+FLOPS = 2 * ROWS * C * N
+
+
+def row_scale(m):
+    if m < C // P:
+        return SCALE
+    if m == QKV // P:
+        return SCALE_L
+    return 1.0
+
+
+def tile_differentialwindowattention_b_kernel(tc, x, qkv_w, qkv_b, ql_w, kl_w, vl_w, offs, out):
+    nc = tc.nc
+    with (
+        tc.tile_pool(name="held", bufs=1) as held,
+        tc.tile_pool(name="picked", bufs=4) as picked,
+        tc.tile_pool(name="staged", bufs=6) as staged,
+        tc.psum_pool(name="psum", bufs=BANKS) as psum,
+    ):
+        offsets = held.tile([P, N // 16], U16, name="offsets")
+        nc.sync.dma_start(offsets[:], offs)
+
+        weights = held.tile([P, KB, ROWS], BF16, name="weights")
+        first_rows = BANKS * P
+        qkv_blocks = qkv_w.rearrange("(k p) r -> p k r", p=P)
+        nc.sync.dma_start(weights[:, :, 0:first_rows], qkv_blocks[:, :, 0:first_rows])
+
+        x_block = [held.tile([P, S], F32, name="x%d" % k) for k in range(KB)]
+        for k in range(KB):
+            nc.sync.dma_start(x_block[k][:], x[k * P:(k + 1) * P, :])
+
+        nc.sync.dma_start(weights[:, :, first_rows:QKV], qkv_blocks[:, :, first_rows:QKV])
+        for i, small_w in enumerate((ql_w, kl_w, vl_w)):
+            nc.sync.dma_start(
+                weights[:, :, QKV + i * LD:QKV + (i + 1) * LD],
+                small_w.rearrange("(k p) r -> p k r", p=P),
+            )
+
+        bias = held.tile([P, MB], F32, name="bias")
+        nc.vector.memset(bias[:], 0.0)
+        with nc.allow_non_contiguous_dma(reason="one bias value to a partition"):
+            nc.scalar.dma_start(bias[:, 0:QKV // P], qkv_b.rearrange("(m p) o -> p (m o)", p=P))
+        nc.vector.tensor_scalar_mul(bias[:, 0:C // P], bias[:, 0:C // P], SCALE)
+
+        xp = [held.tile([P, N], BF16, name="xp%d" % k) for k in range(KB)]
+
+        def pick(k, n):
+            columns = picked.tile([P, CHUNK], F32, name="columns")
+            piece = offsets[:, n * (CHUNK // 16):(n + 1) * (CHUNK // 16)]
+            nc.scalar.activation(columns[:], x_block[k][:].indirect(piece), COPY)
+            nc.vector.tensor_copy(xp[k][:, n * CHUNK:(n + 1) * CHUNK], columns[:])
+
+        def multiply(acc, m, n, k):
+            nc.tensor.matmul(
+                acc[:],
+                weights[:, k, m * P:(m + 1) * P],
+                xp[k][:, n * CHUNK:(n + 1) * CHUNK],
+                start=(k == 0),
+                stop=(k == KB - 1),
+            )
+
+        def finish(acc, m, n):
+            result = staged.tile([P, CHUNK], F32, name="result")
+            if m % 3 == 2:
+                nc.scalar.activation(result[:], acc[:], IDENTITY, bias=bias[:, m:m + 1], scale=row_scale(m))
+            else:
+                nc.vector.tensor_scalar(result[:], acc[:], row_scale(m), bias[:, m:m + 1], MULT, ADD)
+            nc.sync.dma_start(out[m * P:(m + 1) * P, n * CHUNK:(n + 1) * CHUNK], result[:])
+
+        first = [psum.tile([P, CHUNK], F32, name="acc") for m in range(BANKS)]
+        for k in range(KB):
+            pick(k, 0)
+            for m in range(BANKS):
+                multiply(first[m], m, 0, k)
+            pick(k, 1)
+        for m in range(BANKS):
+            finish(first[m], m, 0)
+
+        for n in range(NCH):
+            if 1 <= n < NCH - 1:
+                for k in range(KB):
+                    pick(k, n + 1)
+            for m in range(BANKS if n == 0 else 0, MB):
+                acc = psum.tile([P, CHUNK], F32, name="acc")
+                for k in range(KB):
+                    multiply(acc, m, n, k)
+                finish(acc, m, n)

@@ -17,11 +17,16 @@ LD = 128
 ROWS = QKV + 3 * LD
 KB = C // P
 MB = ROWS // P
+MAIN = QKV // P
 CHUNK = 512
 NCH = N // CHUNK
 BANKS = 8
 SCALE = 32 ** -0.5
 SCALE_L = 8 ** -0.5
+
+ALL_BLOCKS = (0, 1, 2, 3)
+EARLY_BLOCKS = (0, 1)
+LATE_BLOCKS = (2, 3)
 
 FLOPS = 2 * ROWS * C * N
 
@@ -29,7 +34,7 @@ FLOPS = 2 * ROWS * C * N
 def row_scale(m):
     if m < C // P:
         return SCALE
-    if m == QKV // P:
+    if m == MAIN:
         return SCALE_L
     return 1.0
 
@@ -39,35 +44,36 @@ def tile_differentialwindowattention_b_kernel(tc, x, qkv_w, qkv_b, ql_w, kl_w, v
     with (
         tc.tile_pool(name="held", bufs=1) as held,
         tc.tile_pool(name="picked", bufs=4) as picked,
-        tc.tile_pool(name="staged", bufs=6) as staged,
+        tc.tile_pool(name="staged", bufs=8) as staged,
         tc.psum_pool(name="psum", bufs=BANKS) as psum,
     ):
         offsets = held.tile([P, N // 16], U16, name="offsets")
-        nc.sync.dma_start(offsets[:], offs)
-
-        weights = held.tile([P, KB, ROWS], BF16, name="weights")
-        first_rows = BANKS * P
-        qkv_blocks = qkv_w.rearrange("(k p) r -> p k r", p=P)
-        nc.sync.dma_start(weights[:, :, 0:first_rows], qkv_blocks[:, :, 0:first_rows])
-
         x_block = [held.tile([P, S], F32, name="x%d" % k) for k in range(KB)]
-        for k in range(KB):
-            nc.sync.dma_start(x_block[k][:], x[k * P:(k + 1) * P, :])
-
-        nc.sync.dma_start(weights[:, :, first_rows:QKV], qkv_blocks[:, :, first_rows:QKV])
-        for i, small_w in enumerate((ql_w, kl_w, vl_w)):
-            nc.sync.dma_start(
-                weights[:, :, QKV + i * LD:QKV + (i + 1) * LD],
-                small_w.rearrange("(k p) r -> p k r", p=P),
-            )
-
+        w_main = held.tile([P, KB, QKV], BF16, name="w_main")
+        w_small = held.tile([P, 3, KB, LD], BF16, name="w_small")
         bias = held.tile([P, MB], F32, name="bias")
+
+        x_blocks = x.rearrange("(p k) s -> p k s", k=KB)
+        qkv_blocks = qkv_w.rearrange("(p k) r -> p k r", k=KB)
+
+        nc.sync.dma_start(offsets[:], offs)
+        nc.sync.dma_start(x_block[0][:], x_blocks[:, 0, :])
+        nc.sync.dma_start(w_main[:, 0:2, :], qkv_blocks[:, 0:2, :])
+        nc.sync.dma_start(x_block[1][:], x_blocks[:, 1, :])
+        nc.sync.dma_start(w_main[:, 2, :], qkv_blocks[:, 2, :])
+        nc.sync.dma_start(x_block[2][:], x_blocks[:, 2, :])
+        nc.sync.dma_start(x_block[3][:], x_blocks[:, 3, :])
+        nc.sync.dma_start(w_main[:, 3, :], qkv_blocks[:, 3, :])
+
         nc.vector.memset(bias[:], 0.0)
         with nc.allow_non_contiguous_dma(reason="one bias value to a partition"):
-            nc.scalar.dma_start(bias[:, 0:QKV // P], qkv_b.rearrange("(m p) o -> p (m o)", p=P))
-        nc.vector.tensor_scalar_mul(bias[:, 0:C // P], bias[:, 0:C // P], SCALE)
+            nc.scalar.dma_start(bias[:, 0:MAIN], qkv_b.rearrange("(m p) o -> p (m o)", p=P))
+        for i, small in enumerate((ql_w, kl_w, vl_w)):
+            nc.scalar.dma_start(w_small[:, i, :, :], small.rearrange("(p k) r -> p k r", k=KB))
+        nc.scalar.activation(bias[:, 0:C // P], bias[:, 0:C // P], COPY, scale=SCALE)
 
         xp = [held.tile([P, N], BF16, name="xp%d" % k) for k in range(KB)]
+        half = [held.tile([P, CHUNK], F32, name="half%d" % m) for m in range(MB)]
 
         def pick(k, n):
             columns = picked.tile([P, CHUNK], F32, name="columns")
@@ -75,38 +81,54 @@ def tile_differentialwindowattention_b_kernel(tc, x, qkv_w, qkv_b, ql_w, kl_w, v
             nc.scalar.activation(columns[:], x_block[k][:].indirect(piece), COPY)
             nc.vector.tensor_copy(xp[k][:, n * CHUNK:(n + 1) * CHUNK], columns[:])
 
-        def multiply(acc, m, n, k):
-            nc.tensor.matmul(
-                acc[:],
-                weights[:, k, m * P:(m + 1) * P],
-                xp[k][:, n * CHUNK:(n + 1) * CHUNK],
-                start=(k == 0),
-                stop=(k == KB - 1),
-            )
+        def product(m, n, blocks):
+            acc = psum.tile([P, CHUNK], F32, name="acc")
+            for k in blocks:
+                nc.tensor.matmul(
+                    acc[:],
+                    w_main[:, k, m * P:(m + 1) * P] if m < MAIN else w_small[:, m - MAIN, k, :],
+                    xp[k][:, n * CHUNK:(n + 1) * CHUNK],
+                    start=(k == blocks[0]),
+                    stop=(k == blocks[-1]),
+                )
+            return acc
 
-        def finish(acc, m, n):
-            result = staged.tile([P, CHUNK], F32, name="result")
-            if m % 3 == 2:
-                nc.scalar.activation(result[:], acc[:], IDENTITY, bias=bias[:, m:m + 1], scale=row_scale(m))
+        def scale_and_bias(dest, acc, m, on_scalar):
+            if on_scalar:
+                nc.scalar.activation(dest[:], acc[:], IDENTITY, bias=bias[:, m:m + 1], scale=row_scale(m))
             else:
-                nc.vector.tensor_scalar(result[:], acc[:], row_scale(m), bias[:, m:m + 1], MULT, ADD)
+                nc.vector.tensor_scalar(dest[:], acc[:], row_scale(m), bias[:, m:m + 1], MULT, ADD)
+
+        def store(result, m, n):
             nc.sync.dma_start(out[m * P:(m + 1) * P, n * CHUNK:(n + 1) * CHUNK], result[:])
 
-        first = [psum.tile([P, CHUNK], F32, name="acc") for m in range(BANKS)]
-        for k in range(KB):
-            pick(k, 0)
-            for m in range(BANKS):
-                multiply(first[m], m, 0, k)
-            pick(k, 1)
-        for m in range(BANKS):
-            finish(first[m], m, 0)
+        def whole_tile(m, n, on_scalar):
+            acc = product(m, n, ALL_BLOCKS)
+            result = staged.tile([P, CHUNK], F32, name="result")
+            scale_and_bias(result, acc, m, on_scalar)
+            store(result, m, n)
 
-        for n in range(NCH):
-            if 1 <= n < NCH - 1:
-                for k in range(KB):
-                    pick(k, n + 1)
-            for m in range(BANKS if n == 0 else 0, MB):
-                acc = psum.tile([P, CHUNK], F32, name="acc")
-                for k in range(KB):
-                    multiply(acc, m, n, k)
-                finish(acc, m, n)
+        for k in EARLY_BLOCKS:
+            pick(k, 0)
+        for k in ALL_BLOCKS:
+            pick(k, 1)
+        for m in range(MB):
+            scale_and_bias(half[m], product(m, 0, EARLY_BLOCKS), m, on_scalar=(m % 3 == 2))
+
+        later = [(k, 0) for k in LATE_BLOCKS] + [(k, 2) for k in ALL_BLOCKS]
+        for m in range(MB):
+            if m < len(later):
+                pick(later[m][0], later[m][1])
+            whole_tile(m, 1, on_scalar=(m % 2 == 1))
+
+        for m in range(MB):
+            if m < KB:
+                pick(m, 3)
+            acc = product(m, 0, LATE_BLOCKS)
+            result = staged.tile([P, CHUNK], F32, name="result")
+            nc.vector.scalar_tensor_tensor(result[:], acc[:], row_scale(m), half[m][:], MULT, ADD)
+            store(result, m, 0)
+            whole_tile(m, 2, on_scalar=True)
+
+        for m in range(MB):
+            whole_tile(m, 3, on_scalar=(m % 2 == 1))

@@ -25,8 +25,9 @@ SCALE = 32 ** -0.5
 SCALE_L = 8 ** -0.5
 
 ALL_BLOCKS = (0, 1, 2, 3)
-EARLY_BLOCKS = (0, 1)
-LATE_BLOCKS = (2, 3)
+SPLIT_CHUNKS = (0, 1)
+FIRST_PART = ((0,), (0, 1))
+SECOND_PART = ((1, 2, 3), (2, 3))
 
 FLOPS = 2 * ROWS * C * N
 
@@ -57,23 +58,19 @@ def tile_differentialwindowattention_b_kernel(tc, x, qkv_w, qkv_b, ql_w, kl_w, v
         qkv_blocks = qkv_w.rearrange("(p k) r -> p k r", k=KB)
 
         nc.sync.dma_start(offsets[:], offs)
-        nc.sync.dma_start(x_block[0][:], x_blocks[:, 0, :])
-        nc.sync.dma_start(w_main[:, 0:2, :], qkv_blocks[:, 0:2, :])
-        nc.sync.dma_start(x_block[1][:], x_blocks[:, 1, :])
-        nc.sync.dma_start(w_main[:, 2, :], qkv_blocks[:, 2, :])
-        nc.sync.dma_start(x_block[2][:], x_blocks[:, 2, :])
-        nc.sync.dma_start(x_block[3][:], x_blocks[:, 3, :])
-        nc.sync.dma_start(w_main[:, 3, :], qkv_blocks[:, 3, :])
+        for k in range(KB):
+            nc.sync.dma_start(x_block[k][:], x_blocks[:, k, :])
+            nc.sync.dma_start(w_main[:, k, :], qkv_blocks[:, k, :])
+        for i, small in enumerate((ql_w, kl_w, vl_w)):
+            nc.sync.dma_start(w_small[:, i, :, :], small.rearrange("(p k) r -> p k r", k=KB))
 
         nc.vector.memset(bias[:], 0.0)
         with nc.allow_non_contiguous_dma(reason="one bias value to a partition"):
             nc.scalar.dma_start(bias[:, 0:MAIN], qkv_b.rearrange("(m p) o -> p (m o)", p=P))
-        for i, small in enumerate((ql_w, kl_w, vl_w)):
-            nc.scalar.dma_start(w_small[:, i, :, :], small.rearrange("(p k) r -> p k r", k=KB))
         nc.scalar.activation(bias[:, 0:C // P], bias[:, 0:C // P], COPY, scale=SCALE)
 
         xp = [held.tile([P, N], BF16, name="xp%d" % k) for k in range(KB)]
-        half = [held.tile([P, CHUNK], F32, name="half%d" % m) for m in range(MB)]
+        part = [[held.tile([P, CHUNK], F32, name="part%d_%d" % (n, m)) for m in range(MAIN)] for n in SPLIT_CHUNKS]
 
         def pick(k, n):
             columns = picked.tile([P, CHUNK], F32, name="columns")
@@ -108,27 +105,28 @@ def tile_differentialwindowattention_b_kernel(tc, x, qkv_w, qkv_b, ql_w, kl_w, v
             scale_and_bias(result, acc, m, on_scalar)
             store(result, m, n)
 
-        for k in EARLY_BLOCKS:
-            pick(k, 0)
+        for n in SPLIT_CHUNKS:
+            for k in FIRST_PART[n]:
+                pick(k, n)
         for k in ALL_BLOCKS:
-            pick(k, 1)
-        for m in range(MB):
-            scale_and_bias(half[m], product(m, 0, EARLY_BLOCKS), m, on_scalar=(m % 3 == 2))
+            pick(k, 2)
+        for n in SPLIT_CHUNKS:
+            for m in range(MAIN):
+                scale_and_bias(part[n][m], product(m, n, FIRST_PART[n]), m, on_scalar=(m % 2 == 1))
 
-        later = [(k, 0) for k in LATE_BLOCKS] + [(k, 2) for k in ALL_BLOCKS]
+        later = [(k, n) for n in SPLIT_CHUNKS for k in SECOND_PART[n]] + [(k, 3) for k in ALL_BLOCKS]
         for m in range(MB):
             if m < len(later):
                 pick(later[m][0], later[m][1])
-            whole_tile(m, 1, on_scalar=(m % 2 == 1))
+            whole_tile(m, 2, on_scalar=(m % 3 == 2))
 
         for m in range(MB):
-            if m < KB:
-                pick(m, 3)
-            acc = product(m, 0, LATE_BLOCKS)
-            result = staged.tile([P, CHUNK], F32, name="result")
-            nc.vector.scalar_tensor_tensor(result[:], acc[:], row_scale(m), half[m][:], MULT, ADD)
-            store(result, m, 0)
-            whole_tile(m, 2, on_scalar=True)
-
-        for m in range(MB):
-            whole_tile(m, 3, on_scalar=(m % 2 == 1))
+            for n in SPLIT_CHUNKS:
+                if m < MAIN:
+                    acc = product(m, n, SECOND_PART[n])
+                    result = staged.tile([P, CHUNK], F32, name="result")
+                    nc.vector.scalar_tensor_tensor(result[:], acc[:], row_scale(m), part[n][m][:], MULT, ADD)
+                    store(result, m, n)
+                else:
+                    whole_tile(m, n, on_scalar=False)
+            whole_tile(m, 3, on_scalar=True)

@@ -52,10 +52,14 @@ def tile_differentialwindowattention_b_kernel(tc, x, qkv_w, qkv_b, ql_w, kl_w, v
         x_block = [held.tile([P, S], F32, name="x%d" % k) for k in range(KB)]
         w_main = held.tile([P, KB, QKV], BF16, name="w_main")
         w_small = held.tile([P, 3, KB, LD], BF16, name="w_small")
-        bias = held.tile([P, MB], F32, name="bias")
+        bias = held.tile([P, MAIN], F32, name="bias")
+        no_bias = held.tile([P, 1], F32, name="no_bias")
 
         x_blocks = x.rearrange("(p k) s -> p k s", k=KB)
         qkv_blocks = qkv_w.rearrange("(p k) r -> p k r", k=KB)
+
+        with nc.allow_non_contiguous_dma(reason="one bias value to a partition"):
+            nc.scalar.dma_start(bias[:], qkv_b.rearrange("(m p) o -> p (m o)", p=P))
 
         nc.sync.dma_start(offsets[:], offs)
         for k in range(KB):
@@ -64,10 +68,8 @@ def tile_differentialwindowattention_b_kernel(tc, x, qkv_w, qkv_b, ql_w, kl_w, v
         for i, small in enumerate((ql_w, kl_w, vl_w)):
             nc.sync.dma_start(w_small[:, i, :, :], small.rearrange("(p k) r -> p k r", k=KB))
 
-        nc.vector.memset(bias[:], 0.0)
-        with nc.allow_non_contiguous_dma(reason="one bias value to a partition"):
-            nc.scalar.dma_start(bias[:, 0:MAIN], qkv_b.rearrange("(m p) o -> p (m o)", p=P))
         nc.scalar.activation(bias[:, 0:C // P], bias[:, 0:C // P], COPY, scale=SCALE)
+        nc.vector.memset(no_bias[:], 0.0)
 
         xp = [held.tile([P, N], BF16, name="xp%d" % k) for k in range(KB)]
         part = [[held.tile([P, CHUNK], F32, name="part%d_%d" % (n, m)) for m in range(MAIN)] for n in SPLIT_CHUNKS]
@@ -91,10 +93,11 @@ def tile_differentialwindowattention_b_kernel(tc, x, qkv_w, qkv_b, ql_w, kl_w, v
             return acc
 
         def scale_and_bias(dest, acc, m, on_scalar):
+            row_bias = bias[:, m:m + 1] if m < MAIN else no_bias[:]
             if on_scalar:
-                nc.scalar.activation(dest[:], acc[:], IDENTITY, bias=bias[:, m:m + 1], scale=row_scale(m))
+                nc.scalar.activation(dest[:], acc[:], IDENTITY, bias=row_bias, scale=row_scale(m))
             else:
-                nc.vector.tensor_scalar(dest[:], acc[:], row_scale(m), bias[:, m:m + 1], MULT, ADD)
+                nc.vector.tensor_scalar(dest[:], acc[:], row_scale(m), row_bias, MULT, ADD)
 
         def store(result, m, n):
             nc.sync.dma_start(out[m * P:(m + 1) * P, n * CHUNK:(n + 1) * CHUNK], result[:])

@@ -32,6 +32,10 @@ SECOND_PART = ((1, 2, 3), (2, 3))
 FLOPS = 2 * ROWS * C * N
 
 
+def chunk(n):
+    return slice(n * CHUNK, (n + 1) * CHUNK)
+
+
 def row_scale(m):
     if m < C // P:
         return SCALE
@@ -53,23 +57,25 @@ def tile_differentialwindowattention_b_kernel(tc, x, qkv_w, qkv_b, ql_w, kl_w, v
         w_main = held.tile([P, KB, QKV], BF16, name="w_main")
         w_small = held.tile([P, 3, KB, LD], BF16, name="w_small")
         bias = held.tile([P, MAIN], F32, name="bias")
+        zero = held.tile([P, 1], F32, name="zero")
         no_bias = held.tile([P, 1], F32, name="no_bias")
 
         x_blocks = x.rearrange("(p k) s -> p k s", k=KB)
         qkv_blocks = qkv_w.rearrange("(p k) r -> p k r", k=KB)
 
-        with nc.allow_non_contiguous_dma(reason="one bias value to a partition"):
-            nc.scalar.dma_start(bias[:], qkv_b.rearrange("(m p) o -> p (m o)", p=P))
-
         nc.sync.dma_start(offsets[:], offs)
         for k in range(KB):
             nc.sync.dma_start(x_block[k][:], x_blocks[:, k, :])
             nc.sync.dma_start(w_main[:, k, :], qkv_blocks[:, k, :])
+            if k == 0:
+                with nc.allow_non_contiguous_dma(reason="one bias value to a partition"):
+                    nc.sync.dma_start(bias[:], qkv_b.rearrange("(m p) o -> p (m o)", p=P))
         for i, small in enumerate((ql_w, kl_w, vl_w)):
             nc.sync.dma_start(w_small[:, i, :, :], small.rearrange("(p k) r -> p k r", k=KB))
 
-        nc.scalar.activation(bias[:, 0:C // P], bias[:, 0:C // P], COPY, scale=SCALE)
-        nc.vector.memset(no_bias[:], 0.0)
+        nc.vector.memset(zero[:], 0.0)
+        nc.scalar.activation(no_bias[:], zero[:], COPY)
+        nc.vector.tensor_scalar_mul(bias[:, 0:C // P], bias[:, 0:C // P], SCALE)
 
         xp = [held.tile([P, N], BF16, name="xp%d" % k) for k in range(KB)]
         part = [[held.tile([P, CHUNK], F32, name="part%d_%d" % (n, m)) for m in range(MAIN)] for n in SPLIT_CHUNKS]
@@ -78,15 +84,15 @@ def tile_differentialwindowattention_b_kernel(tc, x, qkv_w, qkv_b, ql_w, kl_w, v
             columns = picked.tile([P, CHUNK], F32, name="columns")
             piece = offsets[:, n * (CHUNK // 16):(n + 1) * (CHUNK // 16)]
             nc.scalar.activation(columns[:], x_block[k][:].indirect(piece), COPY)
-            nc.vector.tensor_copy(xp[k][:, n * CHUNK:(n + 1) * CHUNK], columns[:])
+            nc.vector.tensor_copy(xp[k][:, chunk(n)], columns[:])
 
-        def product(m, n, blocks):
-            acc = psum.tile([P, CHUNK], F32, name="acc")
+        def product(m, cols, blocks):
+            acc = psum.tile([P, cols.stop - cols.start], F32, name="acc")
             for k in blocks:
                 nc.tensor.matmul(
                     acc[:],
                     w_main[:, k, m * P:(m + 1) * P] if m < MAIN else w_small[:, m - MAIN, k, :],
-                    xp[k][:, n * CHUNK:(n + 1) * CHUNK],
+                    xp[k][:, cols],
                     start=(k == blocks[0]),
                     stop=(k == blocks[-1]),
                 )
@@ -99,14 +105,14 @@ def tile_differentialwindowattention_b_kernel(tc, x, qkv_w, qkv_b, ql_w, kl_w, v
             else:
                 nc.vector.tensor_scalar(dest[:], acc[:], row_scale(m), row_bias, MULT, ADD)
 
-        def store(result, m, n):
-            nc.sync.dma_start(out[m * P:(m + 1) * P, n * CHUNK:(n + 1) * CHUNK], result[:])
+        def store(result, m, cols):
+            nc.sync.dma_start(out[m * P:(m + 1) * P, cols], result[:])
 
-        def whole_tile(m, n, on_scalar):
-            acc = product(m, n, ALL_BLOCKS)
-            result = staged.tile([P, CHUNK], F32, name="result")
+        def whole_tile(m, cols, on_scalar):
+            acc = product(m, cols, ALL_BLOCKS)
+            result = staged.tile([P, cols.stop - cols.start], F32, name="result")
             scale_and_bias(result, acc, m, on_scalar)
-            store(result, m, n)
+            store(result, m, cols)
 
         for n in SPLIT_CHUNKS:
             for k in FIRST_PART[n]:
@@ -115,21 +121,25 @@ def tile_differentialwindowattention_b_kernel(tc, x, qkv_w, qkv_b, ql_w, kl_w, v
             pick(k, 2)
         for n in SPLIT_CHUNKS:
             for m in range(MAIN):
-                scale_and_bias(part[n][m], product(m, n, FIRST_PART[n]), m, on_scalar=(m % 2 == 1))
+                scale_and_bias(part[n][m], product(m, chunk(n), FIRST_PART[n]), m, on_scalar=(m % 2 == 1))
 
         later = [(k, n) for n in SPLIT_CHUNKS for k in SECOND_PART[n]] + [(k, 3) for k in ALL_BLOCKS]
         for m in range(MB):
             if m < len(later):
                 pick(later[m][0], later[m][1])
-            whole_tile(m, 2, on_scalar=(m % 3 == 2))
+            whole_tile(m, chunk(2), on_scalar=(m % 3 == 2))
 
         for m in range(MB):
             for n in SPLIT_CHUNKS:
                 if m < MAIN:
-                    acc = product(m, n, SECOND_PART[n])
+                    acc = product(m, chunk(n), SECOND_PART[n])
                     result = staged.tile([P, CHUNK], F32, name="result")
                     nc.vector.scalar_tensor_tensor(result[:], acc[:], row_scale(m), part[n][m][:], MULT, ADD)
-                    store(result, m, n)
+                    store(result, m, chunk(n))
                 else:
-                    whole_tile(m, n, on_scalar=False)
-            whole_tile(m, 3, on_scalar=True)
+                    whole_tile(m, chunk(n), on_scalar=False)
+            if m < MB - 1:
+                whole_tile(m, chunk(3), on_scalar=True)
+        middle = 3 * CHUNK + CHUNK // 2
+        whole_tile(MB - 1, slice(3 * CHUNK, middle), on_scalar=True)
+        whole_tile(MB - 1, slice(middle, N), on_scalar=False)

@@ -36,6 +36,11 @@ def chunk(n):
     return slice(n * CHUNK, (n + 1) * CHUNK)
 
 
+def halves(cols):
+    middle = (cols.start + cols.stop) // 2
+    return slice(cols.start, middle), slice(middle, cols.stop)
+
+
 def row_scale(m):
     if m < C // P:
         return SCALE
@@ -80,11 +85,11 @@ def tile_differentialwindowattention_b_kernel(tc, x, qkv_w, qkv_b, ql_w, kl_w, v
         xp = [held.tile([P, N], BF16, name="xp%d" % k) for k in range(KB)]
         part = [[held.tile([P, CHUNK], F32, name="part%d_%d" % (n, m)) for m in range(MAIN)] for n in SPLIT_CHUNKS]
 
-        def pick(k, n):
-            columns = picked.tile([P, CHUNK], F32, name="columns")
-            piece = offsets[:, n * (CHUNK // 16):(n + 1) * (CHUNK // 16)]
+        def pick(k, cols):
+            columns = picked.tile([P, cols.stop - cols.start], F32, name="columns")
+            piece = offsets[:, cols.start // 16:cols.stop // 16]
             nc.scalar.activation(columns[:], x_block[k][:].indirect(piece), COPY)
-            nc.vector.tensor_copy(xp[k][:, chunk(n)], columns[:])
+            nc.vector.tensor_copy(xp[k][:, cols], columns[:])
 
         def product(m, cols, blocks):
             acc = psum.tile([P, cols.stop - cols.start], F32, name="acc")
@@ -96,6 +101,12 @@ def tile_differentialwindowattention_b_kernel(tc, x, qkv_w, qkv_b, ql_w, kl_w, v
                     start=(k == blocks[0]),
                     stop=(k == blocks[-1]),
                 )
+            return acc
+
+        def earliest_product(m):
+            acc = psum.tile([P, CHUNK], F32, name="acc")
+            for half in halves(chunk(0)):
+                nc.tensor.matmul(acc[:, half], w_main[:, 0, m * P:(m + 1) * P], xp[0][:, half], start=True, stop=True)
             return acc
 
         def scale_and_bias(dest, acc, m, on_scalar):
@@ -114,19 +125,21 @@ def tile_differentialwindowattention_b_kernel(tc, x, qkv_w, qkv_b, ql_w, kl_w, v
             scale_and_bias(result, acc, m, on_scalar)
             store(result, m, cols)
 
-        for n in SPLIT_CHUNKS:
-            for k in FIRST_PART[n]:
-                pick(k, n)
+        for half in halves(chunk(0)):
+            pick(0, half)
+        for k in FIRST_PART[1]:
+            pick(k, chunk(1))
         for k in ALL_BLOCKS:
-            pick(k, 2)
-        for n in SPLIT_CHUNKS:
-            for m in range(MAIN):
-                scale_and_bias(part[n][m], product(m, chunk(n), FIRST_PART[n]), m, on_scalar=(m % 2 == 1))
+            pick(k, chunk(2))
+        for m in range(MAIN):
+            scale_and_bias(part[0][m], earliest_product(m), m, on_scalar=(m % 2 == 1))
+        for m in range(MAIN):
+            scale_and_bias(part[1][m], product(m, chunk(1), FIRST_PART[1]), m, on_scalar=(m % 2 == 1))
 
         later = [(k, n) for n in SPLIT_CHUNKS for k in SECOND_PART[n]] + [(k, 3) for k in ALL_BLOCKS]
         for m in range(MB):
             if m < len(later):
-                pick(later[m][0], later[m][1])
+                pick(later[m][0], chunk(later[m][1]))
             whole_tile(m, chunk(2), on_scalar=(m % 3 == 2))
 
         for m in range(MB):
@@ -140,6 +153,6 @@ def tile_differentialwindowattention_b_kernel(tc, x, qkv_w, qkv_b, ql_w, kl_w, v
                     whole_tile(m, chunk(n), on_scalar=False)
             if m < MB - 1:
                 whole_tile(m, chunk(3), on_scalar=True)
-        middle = 3 * CHUNK + CHUNK // 2
-        whole_tile(MB - 1, slice(3 * CHUNK, middle), on_scalar=True)
-        whole_tile(MB - 1, slice(middle, N), on_scalar=False)
+        first_half, second_half = halves(chunk(3))
+        whole_tile(MB - 1, first_half, on_scalar=True)
+        whole_tile(MB - 1, second_half, on_scalar=False)

@@ -132,15 +132,15 @@ def tile_differentialwindowattention_b_kernel(tc, x, qkv_w, qkv_b, ql_w, kl_w, v
         for k in ALL_BLOCKS:
             pick(k, chunk(2))
         for m in range(MAIN):
-            scale_and_bias(part[0][m], earliest_product(m), m, on_scalar=(m % 2 == 1))
+            scale_and_bias(part[0][m], earliest_product(m), m, on_scalar=(m % 2 == 1 and m < BANKS))
         for m in range(MAIN):
-            scale_and_bias(part[1][m], product(m, chunk(1), FIRST_PART[1]), m, on_scalar=(m % 2 == 1))
+            scale_and_bias(part[1][m], product(m, chunk(1), FIRST_PART[1]), m, on_scalar=(m % 2 == 1 and m < BANKS))
 
         later = [(k, n) for n in SPLIT_CHUNKS for k in SECOND_PART[n]] + [(k, 3) for k in ALL_BLOCKS]
         for m in range(MB):
             if m < len(later):
                 pick(later[m][0], chunk(later[m][1]))
-            whole_tile(m, chunk(2), on_scalar=(m % 3 == 2))
+            whole_tile(m, chunk(2), on_scalar=(m >= len(later)))
 
         for m in range(MB):
             for n in SPLIT_CHUNKS:

@@ -25,9 +25,10 @@ SCALE = 32 ** -0.5
 SCALE_L = 8 ** -0.5
 
 ALL_BLOCKS = (0, 1, 2, 3)
-SPLIT_CHUNKS = (0, 1)
-FIRST_PART = ((0,), (0, 1))
-SECOND_PART = ((1, 2, 3), (2, 3))
+SPLIT_CHUNKS = (0, 1, 2)
+FIRST_PART = ((0,), (0, 1), (0, 1, 2))
+SECOND_PART = ((1, 2, 3), (2, 3), (3,))
+SPLIT_ROWS = (MAIN, MAIN, MAIN - BANKS)
 
 FLOPS = 2 * ROWS * C * N
 
@@ -83,7 +84,10 @@ def tile_differentialwindowattention_b_kernel(tc, x, qkv_w, qkv_b, ql_w, kl_w, v
         nc.vector.tensor_scalar_mul(bias[:, 0:C // P], bias[:, 0:C // P], SCALE)
 
         xp = [held.tile([P, N], BF16, name="xp%d" % k) for k in range(KB)]
-        part = [[held.tile([P, CHUNK], F32, name="part%d_%d" % (n, m)) for m in range(MAIN)] for n in SPLIT_CHUNKS]
+        part = [
+            [held.tile([P, CHUNK], F32, name="part%d_%d" % (n, m)) for m in range(SPLIT_ROWS[n])]
+            for n in SPLIT_CHUNKS
+        ]
 
         def pick(k, cols):
             columns = picked.tile([P, cols.stop - cols.start], F32, name="columns")
@@ -133,23 +137,24 @@ def tile_differentialwindowattention_b_kernel(tc, x, qkv_w, qkv_b, ql_w, kl_w, v
             pick(k, chunk(2))
         for m in range(MAIN):
             scale_and_bias(part[0][m], earliest_product(m), m, on_scalar=(m % 2 == 1 and m < BANKS))
-        for m in range(MAIN):
-            scale_and_bias(part[1][m], product(m, chunk(1), FIRST_PART[1]), m, on_scalar=(m % 2 == 1 and m < BANKS))
+        for n in (1, 2):
+            for m in range(SPLIT_ROWS[n]):
+                scale_and_bias(part[n][m], product(m, chunk(n), FIRST_PART[n]), m, on_scalar=(m % 2 == 1 and m < BANKS))
 
-        later = [(k, n) for n in SPLIT_CHUNKS for k in SECOND_PART[n]] + [(k, 3) for k in ALL_BLOCKS]
-        for m in range(MB):
-            if m < len(later):
-                pick(later[m][0], chunk(later[m][1]))
-            whole_tile(m, chunk(2), on_scalar=(m >= len(later)))
+        later = [(k, n) for n in (0, 1) for k in SECOND_PART[n]] + [(k, 3) for k in ALL_BLOCKS]
+        for i, m in enumerate(range(SPLIT_ROWS[2], MB)):
+            if i < len(later):
+                pick(later[i][0], chunk(later[i][1]))
+            whole_tile(m, chunk(2), on_scalar=(i >= len(later)))
 
         for m in range(MB):
             for n in SPLIT_CHUNKS:
-                if m < MAIN:
+                if m < SPLIT_ROWS[n]:
                     acc = product(m, chunk(n), SECOND_PART[n])
                     result = staged.tile([P, CHUNK], F32, name="result")
                     nc.vector.scalar_tensor_tensor(result[:], acc[:], row_scale(m), part[n][m][:], MULT, ADD)
                     store(result, m, chunk(n))
-                else:
+                elif n < 2:
                     whole_tile(m, chunk(n), on_scalar=False)
             if m < MB - 1:
                 whole_tile(m, chunk(3), on_scalar=True)

@@ -107,12 +107,6 @@ def tile_differentialwindowattention_b_kernel(tc, x, qkv_w, qkv_b, ql_w, kl_w, v
                 )
             return acc
 
-        def earliest_product(m):
-            acc = psum.tile([P, CHUNK], F32, name="acc")
-            for half in halves(chunk(0)):
-                nc.tensor.matmul(acc[:, half], w_main[:, 0, m * P:(m + 1) * P], xp[0][:, half], start=True, stop=True)
-            return acc
-
         def scale_and_bias(dest, acc, m, on_scalar):
             row_bias = bias[:, m:m + 1] if m < MAIN else no_bias[:]
             if on_scalar:
@@ -129,15 +123,12 @@ def tile_differentialwindowattention_b_kernel(tc, x, qkv_w, qkv_b, ql_w, kl_w, v
             scale_and_bias(result, acc, m, on_scalar)
             store(result, m, cols)
 
-        for half in halves(chunk(0)):
-            pick(0, half)
+        pick(0, chunk(0))
         for k in FIRST_PART[1]:
             pick(k, chunk(1))
         for k in ALL_BLOCKS:
             pick(k, chunk(2))
-        for m in range(MAIN):
-            scale_and_bias(part[0][m], earliest_product(m), m, on_scalar=(m % 2 == 1 and m < BANKS))
-        for n in (1, 2):
+        for n in SPLIT_CHUNKS:
             for m in range(SPLIT_ROWS[n]):
                 scale_and_bias(part[n][m], product(m, chunk(n), FIRST_PART[n]), m, on_scalar=(m % 2 == 1 and m < BANKS))
 

@@ -66,8 +66,8 @@ def tile_differentialwindowattention_b_kernel(tc, x, qkv_w, qkv_b, ql_w, kl_w, v
         zero = held.tile([P, 1], F32, name="zero")
         no_bias = held.tile([P, 1], F32, name="no_bias")
 
-        x_blocks = x.rearrange("(p k) s -> p k s", k=KB)
-        qkv_blocks = qkv_w.rearrange("(p k) r -> p k r", k=KB)
+        x_blocks = x.rearrange("(k p) s -> p k s", p=P)
+        qkv_blocks = qkv_w.rearrange("(k p) r -> p k r", p=P)
 
         nc.sync.dma_start(offsets[:], offs)
         for k in range(KB):
@@ -77,7 +77,7 @@ def tile_differentialwindowattention_b_kernel(tc, x, qkv_w, qkv_b, ql_w, kl_w, v
                 with nc.allow_non_contiguous_dma(reason="one bias value to a partition"):
                     nc.sync.dma_start(bias[:], qkv_b.rearrange("(m p) o -> p (m o)", p=P))
         for i, small in enumerate((ql_w, kl_w, vl_w)):
-            nc.sync.dma_start(w_small[:, i, :, :], small.rearrange("(p k) r -> p k r", k=KB))
+            nc.sync.dma_start(w_small[:, i, :, :], small.rearrange("(k p) r -> p k r", p=P))
 
         nc.vector.memset(zero[:], 0.0)
         nc.scalar.activation(no_bias[:], zero[:], COPY)

import concourse.mybir as mybir

F32 = mybir.dt.float32
BF16 = mybir.dt.bfloat16
U16 = mybir.dt.uint16
COPY = mybir.ActivationFunctionType.Copy
IDENTITY = mybir.ActivationFunctionType.Identity
MULT = mybir.AluOpType.mult
ADD = mybir.AluOpType.add

P = 128
C = 512
S = 4096
N = 2048
QKV = 1536
LD = 128
ROWS = QKV + 3 * LD
KB = C // P
MB = ROWS // P
MAIN = QKV // P
CHUNK = 512
NCH = N // CHUNK
BANKS = 8
SCALE = 32 ** -0.5
SCALE_L = 8 ** -0.5

ALL_BLOCKS = (0, 1, 2, 3)
SPLIT_CHUNKS = (0, 1, 2)
FIRST_PART = ((0,), (0, 1), (0, 1, 2))
SECOND_PART = ((1, 2, 3), (2, 3), (3,))
SPLIT_ROWS = (MAIN, MAIN, MAIN - BANKS)

FLOPS = 2 * ROWS * C * N


def chunk(n):
    return slice(n * CHUNK, (n + 1) * CHUNK)


def halves(cols):
    middle = (cols.start + cols.stop) // 2
    return slice(cols.start, middle), slice(middle, cols.stop)


def row_scale(m):
    if m < C // P:
        return SCALE
    if m == MAIN:
        return SCALE_L
    return 1.0


def tile_differentialwindowattention_b_kernel(tc, x, qkv_w, qkv_b, ql_w, kl_w, vl_w, offs, out):
    nc = tc.nc
    with (
        tc.tile_pool(name="held", bufs=1) as held,
        tc.tile_pool(name="picked", bufs=4) as picked,
        tc.tile_pool(name="staged", bufs=8) as staged,
        tc.psum_pool(name="psum", bufs=BANKS) as psum,
    ):
        offsets = held.tile([P, N // 16], U16, name="offsets")
        x_block = [held.tile([P, S], F32, name="x%d" % k) for k in range(KB)]
        w_main = held.tile([P, KB, QKV], BF16, name="w_main")
        w_small = held.tile([P, 3, KB, LD], BF16, name="w_small")
        bias = held.tile([P, MAIN], F32, name="bias")
        zero = held.tile([P, 1], F32, name="zero")
        no_bias = held.tile([P, 1], F32, name="no_bias")

        x_blocks = x.rearrange("(k p) s -> p k s", p=P)
        qkv_blocks = qkv_w.rearrange("(k p) r -> p k r", p=P)

        nc.sync.dma_start(offsets[:], offs)
        for k in range(KB):
            nc.sync.dma_start(x_block[k][:], x_blocks[:, k, :])
            nc.sync.dma_start(w_main[:, k, :], qkv_blocks[:, k, :])
            if k == 0:
                with nc.allow_non_contiguous_dma(reason="one bias value to a partition"):
                    nc.sync.dma_start(bias[:], qkv_b.rearrange("(m p) o -> p (m o)", p=P))
        for i, small in enumerate((ql_w, kl_w, vl_w)):
            nc.sync.dma_start(w_small[:, i, :, :], small.rearrange("(k p) r -> p k r", p=P))

        nc.vector.memset(zero[:], 0.0)
        nc.scalar.activation(no_bias[:], zero[:], COPY)
        nc.vector.tensor_scalar_mul(bias[:, 0:C // P], bias[:, 0:C // P], SCALE)

        xp = [held.tile([P, N], BF16, name="xp%d" % k) for k in range(KB)]
        part = [
            [held.tile([P, CHUNK], F32, name="part%d_%d" % (n, m)) for m in range(SPLIT_ROWS[n])]
            for n in SPLIT_CHUNKS
        ]

        def pick(k, cols):
            columns = picked.tile([P, cols.stop - cols.start], F32, name="columns")
            piece = offsets[:, cols.start // 16:cols.stop // 16]
            nc.scalar.activation(columns[:], x_block[k][:].indirect(piece), COPY)
            nc.vector.tensor_copy(xp[k][:, cols], columns[:])

        def product(m, cols, blocks):
            acc = psum.tile([P, cols.stop - cols.start], F32, name="acc")
            for k in blocks:
                nc.tensor.matmul(
                    acc[:],
                    w_main[:, k, m * P:(m + 1) * P] if m < MAIN else w_small[:, m - MAIN, k, :],
                    xp[k][:, cols],
                    start=(k == blocks[0]),
                    stop=(k == blocks[-1]),
                )
            return acc

        def scale_and_bias(dest, acc, m, on_scalar):
            row_bias = bias[:, m:m + 1] if m < MAIN else no_bias[:]
            if on_scalar:
                nc.scalar.activation(dest[:], acc[:], IDENTITY, bias=row_bias, scale=row_scale(m))
            else:
                nc.vector.tensor_scalar(dest[:], acc[:], row_scale(m), row_bias, MULT, ADD)

        def store(result, m, cols):
            nc.sync.dma_start(out[m * P:(m + 1) * P, cols], result[:])

        def whole_tile(m, cols, on_scalar):
            acc = product(m, cols, ALL_BLOCKS)
            result = staged.tile([P, cols.stop - cols.start], F32, name="result")
            scale_and_bias(result, acc, m, on_scalar)
            store(result, m, cols)

        pick(0, chunk(0))
        for k in FIRST_PART[1]:
            pick(k, chunk(1))
        for k in ALL_BLOCKS:
            pick(k, chunk(2))
        for n in SPLIT_CHUNKS:
            for m in range(SPLIT_ROWS[n]):
                scale_and_bias(part[n][m], product(m, chunk(n), FIRST_PART[n]), m, on_scalar=(m % 2 == 1 and m < BANKS))

        later = [(k, n) for n in (0, 1) for k in SECOND_PART[n]] + [(k, 3) for k in ALL_BLOCKS]
        for i, m in enumerate(range(SPLIT_ROWS[2], MB)):
            if i < len(later):
                pick(later[i][0], chunk(later[i][1]))
            whole_tile(m, chunk(2), on_scalar=(i >= len(later)))

        for m in range(MB):
            for n in SPLIT_CHUNKS:
                if m < SPLIT_ROWS[n]:
                    acc = product(m, chunk(n), SECOND_PART[n])
                    result = staged.tile([P, CHUNK], F32, name="result")
                    nc.vector.scalar_tensor_tensor(result[:], acc[:], row_scale(m), part[n][m][:], MULT, ADD)
                    store(result, m, chunk(n))
                elif n < 2:
                    whole_tile(m, chunk(n), on_scalar=False)
            if m < MB - 1:
                whole_tile(m, chunk(3), on_scalar=True)
        first_half, second_half = halves(chunk(3))
        whole_tile(MB - 1, first_half, on_scalar=True)
        whole_tile(MB - 1, second_half, on_scalar=False)
